import numpy as np
import ml_dtypes


def mxq(x, axis, fmt="e4m3"):
    dtype, down = {"e4m3": (ml_dtypes.float8_e4m3fn, 7), "e5m2": (ml_dtypes.float8_e5m2, 14)}[fmt]
    v = np.moveaxis(np.asarray(x, np.float32).astype(ml_dtypes.bfloat16).astype(np.float64), axis, -1)
    blocks = v.reshape(v.shape[:-1] + (-1, 32))
    amax = np.abs(blocks).max(-1, keepdims=True)
    byte = np.maximum(np.where(amax > 0, np.frexp(amax)[1] - 1 + 127, 0) - down, 1)
    scale = np.exp2(byte - 127.0)
    codes = (blocks / scale).astype(np.float32).astype(dtype).astype(np.float64)
    return np.moveaxis((codes * scale).reshape(v.shape), -1, axis)


WIDE = False


def mx_kscale(k):
    if not WIDE:
        return np.ones(k)
    levels = np.array([10, -10, 5, -5, 0])
    a = np.random.permutation(np.resize(levels, k // 512 * 4)).reshape(k // 512, 4)
    idx = np.arange(k)
    return np.exp2(a[idx // 512, idx % 128 // 32])


BF16 = ml_dtypes.bfloat16


def bf(x):
    return np.asarray(x, np.float32).astype(BF16)


def f64(x):
    return np.asarray(x).astype(np.float64)


T, D = 4096, 512


def setup_inputs():
    u = mx_kscale(T)
    b0 = np.random.standard_normal(D) * 0.5
    return {"err": bf((np.random.standard_normal((T, D)) * 1.7 + b0) * u[:, None]),
            "train_view": bf(np.random.standard_normal((T, D)) / u[:, None]),
            "test_view": bf(np.random.standard_normal((T, D))),
            "W": bf(np.random.standard_normal((D, D)) / np.sqrt(D)),
            "b": bf(b0),
            "lr_w": bf(np.random.uniform(size=(D, D)) * 0.25 * np.sqrt(T * D)),
            "lr_b": bf(np.random.uniform(size=D) * 0.5 * D / u.max())}


def reference(err, train_view, test_view, W, b, lr_w, lr_b):
    e = f64(err)
    coef = 2.0 / e.size
    gW = coef * (mxq(e, 0, "e4m3").T @ mxq(f64(train_view), 0, "e4m3"))
    gb = coef * e.sum(axis=0)
    W_new = f64(W) - f64(lr_w) * gW
    b_new = f64(b) - f64(lr_b) * gb
    q = f64(test_view)
    return (mxq(q, 1, "e4m3") @ mxq(W_new, 1, "e4m3").T) + b_new + q

@@ -1,0 +1,249 @@
+from contextlib import ExitStack
+
+import concourse.mybir as mybir
+from concourse.masks import make_identity
+
+F32 = mybir.dt.float32
+BF16 = mybir.dt.bfloat16
+U32 = mybir.dt.uint32
+U8 = mybir.dt.uint8
+FP8X4 = mybir.dt.float8_e4m3fn_x4
+ALU = mybir.AluOpType
+ACT = mybir.ActivationFunctionType
+
+P = 128
+PACK = 4
+K_PASS = P * PACK
+TOKENS = 4096
+D = 512
+CHUNKS = TOKENS // K_PASS
+BLOCKS = D // P
+HALVES = 2
+COEF = 2.0 / (TOKENS * D)
+SUM_COLS = 32
+RUN = 4
+
+FLOPS = 2 * 2 * TOKENS * D * D
+
+
+def tile_tttinner_pb_t_kernel(tc, err, train_view, test_view, W, b, lr_w, lr_b, out):
+    nc = tc.nc
+    with ExitStack() as ctx:
+        ctx.enter_context(tc.manual_schedule())
+        keep = ctx.enter_context(tc.tile_pool(name="keep", bufs=1))
+        grouped = ctx.enter_context(tc.tile_pool(name="grouped", bufs=2))
+        q_grouped_pool = ctx.enter_context(tc.tile_pool(name="q_grouped_pool", bufs=BLOCKS))
+        packed = ctx.enter_context(tc.tile_pool(name="packed", bufs=3))
+        work = ctx.enter_context(tc.tile_pool(name="work", bufs=2))
+        z_pool = ctx.enter_context(tc.tile_pool(name="z_pool", bufs=3))
+        mx_psum = ctx.enter_context(tc.psum_pool(name="mx_psum", bufs=4))
+        plain_psum = ctx.enter_context(tc.psum_pool(name="plain_psum", bufs=4))
+
+        def load_rows(source, chunk, name):
+            rows = keep.tile([P, PACK * D], BF16, name="%s%d" % (name, chunk))
+            nc.sync.dma_start(
+                out=rows[:].rearrange("p (j w) -> p j w", j=PACK),
+                in_=source[chunk * K_PASS : (chunk + 1) * K_PASS, :].rearrange("(p j) w -> p j w", j=PACK),
+            )
+            return rows
+
+        tv_rows = []
+        err_rows = []
+        for c in range(CHUNKS):
+            tv_rows.append(load_rows(train_view, c, "tv_rows"))
+            err_rows.append(load_rows(err, c, "err_rows"))
+        lr_sb = keep.tile([P, BLOCKS, D], BF16)
+        nc.sync.dma_start(out=lr_sb[:], in_=lr_w.rearrange("(m p) i -> p m i", p=P))
+        w_sb = keep.tile([P, BLOCKS, D], BF16)
+        nc.sync.dma_start(out=w_sb[:], in_=W.rearrange("(m p) i -> p m i", p=P))
+        q_rows = [load_rows(test_view, g, "q_rows") for g in range(CHUNKS)]
+
+        ident_f32 = keep.tile([P, P], F32)
+        make_identity(nc, ident_f32[:])
+        ident_bf16 = keep.tile([P, P], BF16)
+        make_identity(nc, ident_bf16[:])
+        ones = keep.tile([P, SUM_COLS], BF16)
+        nc.vector.memset(ones[:], 1.0)
+
+        bias_rows = keep.tile([P, P], BF16)
+        nc.vector.memset(bias_rows[:], 0.0)
+        nc.scalar.dma_start(out=bias_rows[0:BLOCKS, :], in_=b.rearrange("(m p) -> m p", p=P))
+        nc.scalar.dma_start(out=bias_rows[BLOCKS : 2 * BLOCKS, :], in_=lr_b.rearrange("(m p) -> m p", p=P))
+        bias_cols_ps = plain_psum.tile([P, P], BF16, tag="plain")
+        nc.tensor.transpose(out=bias_cols_ps[:], in_=bias_rows[:], identity=ident_bf16[:])
+        bias_cols = keep.tile([P, 2 * BLOCKS], F32)
+        nc.vector.tensor_copy(out=bias_cols[:], in_=bias_cols_ps[:, 0 : 2 * BLOCKS])
+
+        grad = [mx_psum.tile([P, D], F32, name="grad%d" % m, tag="mx") for m in range(BLOCKS)]
+        err_sum = plain_psum.tile([P, BLOCKS, SUM_COLS], F32, tag="plain")
+
+        def regroup(engine_copy, rows, name):
+            side_by_side = grouped.tile([P, D, PACK], BF16, name=name, align_bytes=64)
+            engine_copy(
+                out=side_by_side[:].rearrange("p (c i) j -> p c j i", i=RUN),
+                in_=rows[:].rearrange("p (j c i) -> p c j i", j=PACK, i=RUN),
+            )
+            return side_by_side
+
+        def quantise(side_by_side, name):
+            codes = packed.tile([P, D], U32, name=name + "_codes", align_bytes=64)
+            scales = packed.tile([P, D], U8, name=name + "_scales", align_bytes=64)
+            nc.vector.quantize_mx(
+                out=codes[:].bitcast(FP8X4),
+                scales=scales[:],
+                in_=side_by_side[:].rearrange("p w j -> p (w j)"),
+            )
+            return codes, scales
+
+        for c in range(CHUNKS):
+            tv_grouped = regroup(nc.scalar.copy, tv_rows[c], "tv_grouped")
+            err_grouped = regroup(nc.vector.tensor_copy, err_rows[c], "err_grouped")
+            for j in range(PACK):
+                for m in range(BLOCKS):
+                    nc.tensor.matmul(
+                        out=err_sum[:, m, :],
+                        lhsT=err_rows[c][:, j * D + m * P : j * D + (m + 1) * P],
+                        rhs=ones[:],
+                        start=(c == 0 and j == 0 and m == 0),
+                        stop=(c == CHUNKS - 1 and j == PACK - 1 and m == BLOCKS - 1),
+                    )
+            tv_codes, tv_scales = quantise(tv_grouped, "tv")
+            err_codes, err_scales = quantise(err_grouped, "err")
+            for m in range(BLOCKS):
+                o_cols = slice(m * P, (m + 1) * P)
+                nc.tensor.matmul_mx(
+                    out=grad[m][:],
+                    lhsT=err_codes[:, o_cols].bitcast(FP8X4),
+                    lhsT_scale=err_scales[:, o_cols],
+                    rhs=tv_codes[:].bitcast(FP8X4),
+                    rhs_scale=tv_scales[:],
+                    start=(c == 0),
+                    stop=(c == CHUNKS - 1),
+                )
+
+        q_codes = [keep.tile([P, K_PASS], U32, name="q_codes%d" % g, align_bytes=64) for g in range(CHUNKS)]
+        q_scales = [keep.tile([P, K_PASS], U8, name="q_scales%d" % g, align_bytes=64) for g in range(CHUNKS)]
+        q_grouped = {}
+        zT = {}
+
+        def q_transpose(g):
+            words = q_rows[g][:].bitcast(F32)
+            q_grouped[g] = q_grouped_pool.tile([P, PACK * K_PASS], BF16, name="q_grouped", align_bytes=64)
+            grouped_words = q_grouped[g][:].bitcast(F32).rearrange("p (n u) -> p n u", u=HALVES)
+            for h in range(PACK // 2):
+                flipped = plain_psum.tile([P, HALVES, 2 * P], F32, tag="plain")
+                for jj in range(2):
+                    j = 2 * h + jj
+                    for u in range(HALVES):
+                        first_word = (j * HALVES + u) * P
+                        nc.tensor.transpose(
+                            out=flipped[:, u, jj * P : (jj + 1) * P],
+                            in_=words[:, first_word : first_word + P],
+                            identity=ident_f32[:],
+                        )
+                nc.scalar.copy(
+                    out=grouped_words[:, h * 2 * P : (h + 1) * 2 * P, :],
+                    in_=flipped[:].rearrange("p u n -> p n u"),
+                )
+
+        def q_quantise(g):
+            nc.vector.quantize_mx(
+                out=q_codes[g][:].bitcast(FP8X4), scales=q_scales[g][:], in_=q_grouped[g][:]
+            )
+
+        def multiply(g):
+            zT[g] = work.tile([P, BLOCKS, K_PASS], F32, name="zT")
+            for m in range(BLOCKS):
+                o_cols = slice(m * P, (m + 1) * P)
+                product = mx_psum.tile([P, K_PASS], F32, tag="mx")
+                nc.tensor.matmul_mx(
+                    out=product[:],
+                    lhsT=w_codes[:, o_cols].bitcast(FP8X4),
+                    lhsT_scale=w_scales[:, o_cols],
+                    rhs=q_codes[g][:].bitcast(FP8X4),
+                    rhs_scale=q_scales[g][:],
+                    start=True,
+                    stop=True,
+                )
+                nc.scalar.activation(
+                    out=zT[g][:, m, :], in_=product[:], func=ACT.Identity, bias=b_new[:, m : m + 1], scale=1.0
+                )
+
+        def finish(g):
+            z = z_pool.tile([P, PACK, D], F32)
+            for j in range(PACK):
+                back = plain_psum.tile([P, D], F32, tag="plain")
+                for m in range(BLOCKS):
+                    nc.tensor.transpose(
+                        out=back[:, m * P : (m + 1) * P],
+                        in_=zT[g][:, m, j * P : (j + 1) * P],
+                        identity=ident_f32[:],
+                    )
+                nc.vector.tensor_tensor(
+                    out=z[:, j, :], in0=back[:], in1=q_rows[g][:, j * D : (j + 1) * D], op=ALU.add
+                )
+            nc.sync.dma_start(
+                out=out[g * K_PASS : (g + 1) * K_PASS, :].rearrange("(p j) o -> p j o", j=PACK), in_=z[:]
+            )
+
+        w_new = keep.tile([P, BLOCKS, D], BF16)
+        w_grouped = keep.tile([P, BLOCKS, P, PACK], BF16, align_bytes=64)
+        w_codes = keep.tile([P, D], U32, align_bytes=64)
+        w_scales = keep.tile([P, D], U8, align_bytes=64)
+
+        def w_update(m):
+            step = work.tile([P, D], F32, name="step")
+            nc.vector.scalar_tensor_tensor(
+                out=step[:], in0=grad[m][:], scalar=-COEF, in1=lr_sb[:, m, :], op0=ALU.mult, op1=ALU.mult
+            )
+            nc.vector.tensor_tensor(
+                out=w_new[:, m, :].rearrange("p (u e q) -> p u e q", u=HALVES, e=2),
+                in0=step[:].rearrange("p (u q e) -> p u e q", u=HALVES, e=2),
+                in1=w_sb[:, m, :].rearrange("p (u q e) -> p u e q", u=HALVES, e=2),
+                op=ALU.add,
+            )
+            w_flipped = plain_psum.tile([P, PACK, P], BF16, tag="plain")
+            for t in range(PACK):
+                nc.tensor.transpose(
+                    out=w_flipped[:, t, :], in_=w_new[:, m, t * P : (t + 1) * P], identity=ident_bf16[:]
+                )
+            nc.scalar.copy(out=w_grouped[:, m], in_=w_flipped[:].rearrange("p t o -> p o t"))
+
+        def w_quantise(m):
+            o_cols = slice(m * P, (m + 1) * P)
+            nc.vector.quantize_mx(
+                out=w_codes[:, o_cols].bitcast(FP8X4),
+                scales=w_scales[:, o_cols],
+                in_=w_grouped[:, m].rearrange("p o t -> p (o t)"),
+            )
+
+        for m in range(BLOCKS):
+            q_transpose(m)
+            w_update(m)
+            if m > 0:
+                w_quantise(m - 1)
+        w_quantise(BLOCKS - 1)
+
+        bias_step = keep.tile([P, BLOCKS], F32)
+        nc.vector.scalar_tensor_tensor(
+            out=bias_step[:],
+            in0=err_sum[:, :, 0],
+            scalar=-COEF,
+            in1=bias_cols[:, BLOCKS : 2 * BLOCKS],
+            op0=ALU.mult,
+            op1=ALU.mult,
+        )
+        b_new = keep.tile([P, BLOCKS], F32)
+        nc.vector.tensor_tensor(out=b_new[:], in0=bias_step[:], in1=bias_cols[:, 0:BLOCKS], op=ALU.add)
+
+        for g in range(BLOCKS - 1):
+            q_quantise(g)
+        multiply(0)
+        for g in range(CHUNKS):
+            if g + BLOCKS < CHUNKS:
+                q_transpose(g + BLOCKS)
+            if g + BLOCKS - 1 < CHUNKS:
+                q_quantise(g + BLOCKS - 1)
+            if g + 1 < CHUNKS:
+                multiply(g + 1)
+            finish(g)

@@ -69,10 +69,6 @@ def tile_tttinner_pb_t_kernel(tc, err, train_view, test_view, W, b, lr_w, lr_b, 
         nc.vector.memset(bias_rows[:], 0.0)
         nc.scalar.dma_start(out=bias_rows[0:BLOCKS, :], in_=b.rearrange("(m p) -> m p", p=P))
         nc.scalar.dma_start(out=bias_rows[BLOCKS : 2 * BLOCKS, :], in_=lr_b.rearrange("(m p) -> m p", p=P))
-        bias_cols_ps = plain_psum.tile([P, P], BF16, tag="plain")
-        nc.tensor.transpose(out=bias_cols_ps[:], in_=bias_rows[:], identity=ident_bf16[:])
-        bias_cols = keep.tile([P, 2 * BLOCKS], F32)
-        nc.vector.tensor_copy(out=bias_cols[:], in_=bias_cols_ps[:, 0 : 2 * BLOCKS])
 
         grad = [mx_psum.tile([P, D], F32, name="grad%d" % m, tag="mx") for m in range(BLOCKS)]
         err_sum = plain_psum.tile([P, BLOCKS, SUM_COLS], F32, tag="plain")
@@ -126,11 +122,11 @@ def tile_tttinner_pb_t_kernel(tc, err, train_view, test_view, W, b, lr_w, lr_b, 
         q_grouped = {}
         zT = {}
 
-        def q_transpose(g):
+        def q_transpose(g, copy_second_bank):
             words = q_rows[g][:].bitcast(F32)
             q_grouped[g] = q_grouped_pool.tile([P, PACK * K_PASS], BF16, name="q_grouped", align_bytes=64)
             grouped_words = q_grouped[g][:].bitcast(F32).rearrange("p (n u) -> p n u", u=HALVES)
-            for h in range(PACK // 2):
+            for h, copy_out in enumerate([nc.scalar.copy, copy_second_bank]):
                 flipped = plain_psum.tile([P, HALVES, 2 * P], F32, tag="plain")
                 for jj in range(2):
                     j = 2 * h + jj
@@ -141,7 +137,7 @@ def tile_tttinner_pb_t_kernel(tc, err, train_view, test_view, W, b, lr_w, lr_b, 
                             in_=words[:, first_word : first_word + P],
                             identity=ident_f32[:],
                         )
-                nc.scalar.copy(
+                copy_out(
                     out=grouped_words[:, h * 2 * P : (h + 1) * 2 * P, :],
                     in_=flipped[:].rearrange("p u n -> p n u"),
                 )
@@ -171,6 +167,7 @@ def tile_tttinner_pb_t_kernel(tc, err, train_view, test_view, W, b, lr_w, lr_b, 
 
         def finish(g):
             z = z_pool.tile([P, PACK, D], F32)
+            z_rows = out[g * K_PASS : (g + 1) * K_PASS, :].rearrange("(p j) o -> p j o", j=PACK)
             for j in range(PACK):
                 back = plain_psum.tile([P, D], F32, tag="plain")
                 for m in range(BLOCKS):
@@ -182,9 +179,7 @@ def tile_tttinner_pb_t_kernel(tc, err, train_view, test_view, W, b, lr_w, lr_b, 
                 nc.vector.tensor_tensor(
                     out=z[:, j, :], in0=back[:], in1=q_rows[g][:, j * D : (j + 1) * D], op=ALU.add
                 )
-            nc.sync.dma_start(
-                out=out[g * K_PASS : (g + 1) * K_PASS, :].rearrange("(p j) o -> p j o", j=PACK), in_=z[:]
-            )
+                nc.sync.dma_start(out=z_rows[:, j, :], in_=z[:, j, :])
 
         w_new = keep.tile([P, BLOCKS, D], BF16)
         w_grouped = keep.tile([P, BLOCKS, P, PACK], BF16, align_bytes=64)
@@ -218,12 +213,16 @@ def tile_tttinner_pb_t_kernel(tc, err, train_view, test_view, W, b, lr_w, lr_b, 
             )
 
         for m in range(BLOCKS):
-            q_transpose(m)
+            q_transpose(m, nc.scalar.copy)
             w_update(m)
             if m > 0:
                 w_quantise(m - 1)
         w_quantise(BLOCKS - 1)
 
+        bias_cols_ps = plain_psum.tile([P, P], BF16, tag="plain")
+        nc.tensor.transpose(out=bias_cols_ps[:], in_=bias_rows[:], identity=ident_bf16[:])
+        bias_cols = keep.tile([P, 2 * BLOCKS], F32)
+        nc.vector.tensor_copy(out=bias_cols[:], in_=bias_cols_ps[:, 0 : 2 * BLOCKS])
         bias_step = keep.tile([P, BLOCKS], F32)
         nc.vector.scalar_tensor_tensor(
             out=bias_step[:],
@@ -236,14 +235,15 @@ def tile_tttinner_pb_t_kernel(tc, err, train_view, test_view, W, b, lr_w, lr_b, 
         b_new = keep.tile([P, BLOCKS], F32)
         nc.vector.tensor_tensor(out=b_new[:], in0=bias_step[:], in1=bias_cols[:, 0:BLOCKS], op=ALU.add)
 
-        for g in range(BLOCKS - 1):
+        for g in range(BLOCKS):
             q_quantise(g)
         multiply(0)
+        for g in range(BLOCKS, CHUNKS):
+            q_transpose(g, nc.vector.tensor_copy)
+        for g in range(BLOCKS, CHUNKS):
+            q_quantise(g)
+
         for g in range(CHUNKS):
-            if g + BLOCKS < CHUNKS:
-                q_transpose(g + BLOCKS)
-            if g + BLOCKS - 1 < CHUNKS:
-                q_quantise(g + BLOCKS - 1)
             if g + 1 < CHUNKS:
                 multiply(g + 1)
             finish(g)

@@ -22,6 +22,7 @@ HALVES = 2
 COEF = 2.0 / (TOKENS * D)
 SUM_COLS = 32
 RUN = 4
+AHEAD = 2
 
 FLOPS = 2 * 2 * TOKENS * D * D
 
@@ -32,7 +33,6 @@ def tile_tttinner_pb_t_kernel(tc, err, train_view, test_view, W, b, lr_w, lr_b, 
         ctx.enter_context(tc.manual_schedule())
         keep = ctx.enter_context(tc.tile_pool(name="keep", bufs=1))
         grouped = ctx.enter_context(tc.tile_pool(name="grouped", bufs=2))
-        q_grouped_pool = ctx.enter_context(tc.tile_pool(name="q_grouped_pool", bufs=BLOCKS))
         packed = ctx.enter_context(tc.tile_pool(name="packed", bufs=3))
         work = ctx.enter_context(tc.tile_pool(name="work", bufs=2))
         z_pool = ctx.enter_context(tc.tile_pool(name="z_pool", bufs=3))
@@ -40,7 +40,8 @@ def tile_tttinner_pb_t_kernel(tc, err, train_view, test_view, W, b, lr_w, lr_b, 
         plain_psum = ctx.enter_context(tc.psum_pool(name="plain_psum", bufs=4))
 
         def load_rows(source, chunk, name):
-            rows = keep.tile([P, PACK * D], BF16, name="%s%d" % (name, chunk))
+            label = "%s%d" % (name, chunk)
+            rows = keep.tile([P, PACK * D], BF16, name=label, tag=label, align_bytes=64)
             nc.sync.dma_start(
                 out=rows[:].rearrange("p (j w) -> p j w", j=PACK),
                 in_=source[chunk * K_PASS : (chunk + 1) * K_PASS, :].rearrange("(p j) w -> p j w", j=PACK),
@@ -52,11 +53,13 @@ def tile_tttinner_pb_t_kernel(tc, err, train_view, test_view, W, b, lr_w, lr_b, 
         for c in range(CHUNKS):
             tv_rows.append(load_rows(train_view, c, "tv_rows"))
             err_rows.append(load_rows(err, c, "err_rows"))
+        q_rows = [load_rows(test_view, g, "q_rows") for g in range(AHEAD)]
         lr_sb = keep.tile([P, BLOCKS, D], BF16)
         nc.sync.dma_start(out=lr_sb[:], in_=lr_w.rearrange("(m p) i -> p m i", p=P))
         w_sb = keep.tile([P, BLOCKS, D], BF16)
         nc.sync.dma_start(out=w_sb[:], in_=W.rearrange("(m p) i -> p m i", p=P))
-        q_rows = [load_rows(test_view, g, "q_rows") for g in range(CHUNKS)]
+        for g in range(AHEAD, CHUNKS):
+            q_rows.append(load_rows(test_view, g, "q_rows"))
 
         ident_f32 = keep.tile([P, P], F32)
         make_identity(nc, ident_f32[:])
@@ -64,14 +67,21 @@ def tile_tttinner_pb_t_kernel(tc, err, train_view, test_view, W, b, lr_w, lr_b, 
         make_identity(nc, ident_bf16[:])
         ones = keep.tile([P, SUM_COLS], BF16)
         nc.vector.memset(ones[:], 1.0)
+        table_warmer = keep.tile([P, 1], F32)
+        nc.scalar.activation(out=table_warmer[:], in_=ones[:, 0:1], func=ACT.Identity)
 
         bias_rows = keep.tile([P, P], BF16)
         nc.vector.memset(bias_rows[:], 0.0)
         nc.scalar.dma_start(out=bias_rows[0:BLOCKS, :], in_=b.rearrange("(m p) -> m p", p=P))
         nc.scalar.dma_start(out=bias_rows[BLOCKS : 2 * BLOCKS, :], in_=lr_b.rearrange("(m p) -> m p", p=P))
+        bias_cols_ps = plain_psum.tile([P, P], BF16, tag="plain")
+
+        def flip_bias_rows():
+            nc.tensor.transpose(out=bias_cols_ps[:], in_=bias_rows[:], identity=ident_bf16[:])
 
         grad = [mx_psum.tile([P, D], F32, name="grad%d" % m, tag="mx") for m in range(BLOCKS)]
         err_sum = plain_psum.tile([P, BLOCKS, SUM_COLS], F32, tag="plain")
+        operands = {}
 
         def regroup(engine_copy, rows, name):
             side_by_side = grouped.tile([P, D, PACK], BF16, name=name, align_bytes=64)
@@ -91,7 +101,7 @@ def tile_tttinner_pb_t_kernel(tc, err, train_view, test_view, W, b, lr_w, lr_b, 
             )
             return codes, scales
 
-        for c in range(CHUNKS):
+        def prepare(c):
             tv_grouped = regroup(nc.scalar.copy, tv_rows[c], "tv_grouped")
             err_grouped = regroup(nc.vector.tensor_copy, err_rows[c], "err_grouped")
             for j in range(PACK):
@@ -103,8 +113,10 @@ def tile_tttinner_pb_t_kernel(tc, err, train_view, test_view, W, b, lr_w, lr_b, 
                         start=(c == 0 and j == 0 and m == 0),
                         stop=(c == CHUNKS - 1 and j == PACK - 1 and m == BLOCKS - 1),
                     )
-            tv_codes, tv_scales = quantise(tv_grouped, "tv")
-            err_codes, err_scales = quantise(err_grouped, "err")
+            operands[c] = quantise(tv_grouped, "tv") + quantise(err_grouped, "err")
+
+        def gradient(c):
+            tv_codes, tv_scales, err_codes, err_scales = operands[c]
             for m in range(BLOCKS):
                 o_cols = slice(m * P, (m + 1) * P)
                 nc.tensor.matmul_mx(
@@ -117,16 +129,34 @@ def tile_tttinner_pb_t_kernel(tc, err, train_view, test_view, W, b, lr_w, lr_b, 
                     stop=(c == CHUNKS - 1),
                 )
 
+        b_new = keep.tile([P, BLOCKS], F32)
+
+        def update_bias():
+            bias_cols = keep.tile([P, 2 * BLOCKS], F32)
+            nc.vector.tensor_copy(out=bias_cols[:], in_=bias_cols_ps[:, 0 : 2 * BLOCKS])
+            bias_step = keep.tile([P, BLOCKS], F32)
+            nc.vector.scalar_tensor_tensor(
+                out=bias_step[:],
+                in0=err_sum[:, :, 0],
+                scalar=-COEF,
+                in1=bias_cols[:, BLOCKS : 2 * BLOCKS],
+                op0=ALU.mult,
+                op1=ALU.mult,
+            )
+            nc.vector.tensor_tensor(out=b_new[:], in0=bias_step[:], in1=bias_cols[:, 0:BLOCKS], op=ALU.add)
+
         q_codes = [keep.tile([P, K_PASS], U32, name="q_codes%d" % g, align_bytes=64) for g in range(CHUNKS)]
         q_scales = [keep.tile([P, K_PASS], U8, name="q_scales%d" % g, align_bytes=64) for g in range(CHUNKS)]
         q_grouped = {}
         zT = {}
 
-        def q_transpose(g, copy_second_bank):
+        def q_transpose(g):
             words = q_rows[g][:].bitcast(F32)
-            q_grouped[g] = q_grouped_pool.tile([P, PACK * K_PASS], BF16, name="q_grouped", align_bytes=64)
+            q_grouped[g] = keep.tile(
+                [P, PACK * K_PASS], BF16, name="q_grouped%d" % g, tag="tv_rows%d" % g, align_bytes=64
+            )
             grouped_words = q_grouped[g][:].bitcast(F32).rearrange("p (n u) -> p n u", u=HALVES)
-            for h, copy_out in enumerate([nc.scalar.copy, copy_second_bank]):
+            for h in range(PACK // 2):
                 flipped = plain_psum.tile([P, HALVES, 2 * P], F32, tag="plain")
                 for jj in range(2):
                     j = 2 * h + jj
@@ -137,7 +167,7 @@ def tile_tttinner_pb_t_kernel(tc, err, train_view, test_view, W, b, lr_w, lr_b, 
                             in_=words[:, first_word : first_word + P],
                             identity=ident_f32[:],
                         )
-                copy_out(
+                nc.scalar.copy(
                     out=grouped_words[:, h * 2 * P : (h + 1) * 2 * P, :],
                     in_=flipped[:].rearrange("p u n -> p n u"),
                 )
@@ -212,37 +242,30 @@ def tile_tttinner_pb_t_kernel(tc, err, train_view, test_view, W, b, lr_w, lr_b, 
                 in_=w_grouped[:, m].rearrange("p o t -> p (o t)"),
             )
 
+        for c in range(CHUNKS - 1):
+            if c == CHUNKS // 2:
+                flip_bias_rows()
+            prepare(c)
+            gradient(c)
+        prepare(CHUNKS - 1)
+        for g in range(AHEAD):
+            q_transpose(g)
+        gradient(CHUNKS - 1)
+        update_bias()
+
         for m in range(BLOCKS):
-            q_transpose(m, nc.scalar.copy)
+            q_transpose(AHEAD + m)
             w_update(m)
             if m > 0:
                 w_quantise(m - 1)
+        for g in range(AHEAD + BLOCKS, CHUNKS):
+            q_transpose(g)
+        q_quantise(0)
         w_quantise(BLOCKS - 1)
-
-        bias_cols_ps = plain_psum.tile([P, P], BF16, tag="plain")
-        nc.tensor.transpose(out=bias_cols_ps[:], in_=bias_rows[:], identity=ident_bf16[:])
-        bias_cols = keep.tile([P, 2 * BLOCKS], F32)
-        nc.vector.tensor_copy(out=bias_cols[:], in_=bias_cols_ps[:, 0 : 2 * BLOCKS])
-        bias_step = keep.tile([P, BLOCKS], F32)
-        nc.vector.scalar_tensor_tensor(
-            out=bias_step[:],
-            in0=err_sum[:, :, 0],
-            scalar=-COEF,
-            in1=bias_cols[:, BLOCKS : 2 * BLOCKS],
-            op0=ALU.mult,
-            op1=ALU.mult,
-        )
-        b_new = keep.tile([P, BLOCKS], F32)
-        nc.vector.tensor_tensor(out=b_new[:], in0=bias_step[:], in1=bias_cols[:, 0:BLOCKS], op=ALU.add)
-
-        for g in range(BLOCKS):
+        for g in range(1, CHUNKS):
             q_quantise(g)
+
         multiply(0)
-        for g in range(BLOCKS, CHUNKS):
-            q_transpose(g, nc.vector.tensor_copy)
-        for g in range(BLOCKS, CHUNKS):
-            q_quantise(g)
-
         for g in range(CHUNKS):
             if g + 1 < CHUNKS:
                 multiply(g + 1)

@@ -22,7 +22,11 @@ HALVES = 2
 COEF = 2.0 / (TOKENS * D)
 SUM_COLS = 32
 RUN = 4
-AHEAD = 2
+EARLY = 3
+TRANSPOSED = (0, 1, 4, 5)
+LATER = (5, 6, 7)
+SHARES = (3, 2, 4, 4)
+DIRECT = (2, 3, 6, 7)
 
 FLOPS = 2 * 2 * TOKENS * D * D
 
@@ -35,9 +39,21 @@ def tile_tttinner_pb_t_kernel(tc, err, train_view, test_view, W, b, lr_w, lr_b, 
         grouped = ctx.enter_context(tc.tile_pool(name="grouped", bufs=2))
         packed = ctx.enter_context(tc.tile_pool(name="packed", bufs=3))
         work = ctx.enter_context(tc.tile_pool(name="work", bufs=2))
-        z_pool = ctx.enter_context(tc.tile_pool(name="z_pool", bufs=3))
-        mx_psum = ctx.enter_context(tc.psum_pool(name="mx_psum", bufs=4))
-        plain_psum = ctx.enter_context(tc.psum_pool(name="plain_psum", bufs=4))
+        steps = ctx.enter_context(tc.tile_pool(name="steps", bufs=4))
+        z_pool = ctx.enter_context(tc.tile_pool(name="z_pool", bufs=8))
+        rb_pool = ctx.enter_context(tc.tile_pool(name="rb_pool", bufs=16))
+        banks = ctx.enter_context(tc.psum_pool(name="banks", bufs=1))
+        turn = {"plain": 0, "product": 0, "direct": 0}
+        cycle = {"plain": (6, 7, 5), "product": (0, 1, 2), "direct": (3, 4)}
+
+        def bank(number, shape, dtype, name):
+            return banks.tile(shape, dtype, name=name, tag="bank%d" % number)
+
+        def next_bank(kind, shape, dtype, name):
+            numbers = cycle[kind]
+            number = numbers[turn[kind] % len(numbers)]
+            turn[kind] += 1
+            return bank(number, shape, dtype, name)
 
         def load_rows(source, chunk, name):
             label = "%s%d" % (name, chunk)
@@ -50,15 +66,17 @@ def tile_tttinner_pb_t_kernel(tc, err, train_view, test_view, W, b, lr_w, lr_b, 
 
         tv_rows = []
         err_rows = []
+        q_rows = []
         for c in range(CHUNKS):
             tv_rows.append(load_rows(train_view, c, "tv_rows"))
             err_rows.append(load_rows(err, c, "err_rows"))
-        q_rows = [load_rows(test_view, g, "q_rows") for g in range(AHEAD)]
+            if c in (2, 4, 6, 7):
+                q_rows.append(load_rows(test_view, len(q_rows), "q_rows"))
         lr_sb = keep.tile([P, BLOCKS, D], BF16)
         nc.sync.dma_start(out=lr_sb[:], in_=lr_w.rearrange("(m p) i -> p m i", p=P))
         w_sb = keep.tile([P, BLOCKS, D], BF16)
         nc.sync.dma_start(out=w_sb[:], in_=W.rearrange("(m p) i -> p m i", p=P))
-        for g in range(AHEAD, CHUNKS):
+        for g in range(len(q_rows), CHUNKS):
             q_rows.append(load_rows(test_view, g, "q_rows"))
 
         ident_f32 = keep.tile([P, P], F32)
@@ -74,22 +92,27 @@ def tile_tttinner_pb_t_kernel(tc, err, train_view, test_view, W, b, lr_w, lr_b, 
         nc.vector.memset(bias_rows[:], 0.0)
         nc.scalar.dma_start(out=bias_rows[0:BLOCKS, :], in_=b.rearrange("(m p) -> m p", p=P))
         nc.scalar.dma_start(out=bias_rows[BLOCKS : 2 * BLOCKS, :], in_=lr_b.rearrange("(m p) -> m p", p=P))
-        bias_cols_ps = plain_psum.tile([P, P], BF16, tag="plain")
+        bias_cols = keep.tile([P, 2 * BLOCKS], F32)
 
         def flip_bias_rows():
+            bias_cols_ps = next_bank("plain", [P, P], BF16, "bias_cols_ps")
             nc.tensor.transpose(out=bias_cols_ps[:], in_=bias_rows[:], identity=ident_bf16[:])
+            return bias_cols_ps
 
-        grad = [mx_psum.tile([P, D], F32, name="grad%d" % m, tag="mx") for m in range(BLOCKS)]
-        err_sum = plain_psum.tile([P, BLOCKS, SUM_COLS], F32, tag="plain")
+        def copy_bias_cols(bias_cols_ps):
+            nc.vector.tensor_copy(out=bias_cols[:], in_=bias_cols_ps[:, 0 : 2 * BLOCKS])
+
+        grad = [bank(m, [P, D], F32, "grad%d" % m) for m in range(BLOCKS)]
+        err_sum = bank(4, [P, BLOCKS, SUM_COLS], F32, "err_sum")
         operands = {}
 
-        def regroup(engine_copy, rows, name):
-            side_by_side = grouped.tile([P, D, PACK], BF16, name=name, align_bytes=64)
+        def regroup(engine_copy, rows, side_by_side, first, last):
             engine_copy(
-                out=side_by_side[:].rearrange("p (c i) j -> p c j i", i=RUN),
-                in_=rows[:].rearrange("p (j c i) -> p c j i", j=PACK, i=RUN),
+                out=side_by_side[:, first:last, :].rearrange("p (c i) j -> p c j i", i=RUN),
+                in_=rows[:].rearrange("p (j w) -> p j w", j=PACK)[:, :, first:last].rearrange(
+                    "p j (c i) -> p c j i", i=RUN
+                ),
             )
-            return side_by_side
 
         def quantise(side_by_side, name):
             codes = packed.tile([P, D], U32, name=name + "_codes", align_bytes=64)
@@ -101,9 +124,16 @@ def tile_tttinner_pb_t_kernel(tc, err, train_view, test_view, W, b, lr_w, lr_b, 
             )
             return codes, scales
 
-        def prepare(c):
-            tv_grouped = regroup(nc.scalar.copy, tv_rows[c], "tv_grouped")
-            err_grouped = regroup(nc.vector.tensor_copy, err_rows[c], "err_grouped")
+        def regroup_pair(c):
+            tv_grouped = grouped.tile([P, D, PACK], BF16, name="tv_grouped", align_bytes=64)
+            err_grouped = grouped.tile([P, D, PACK], BF16, name="err_grouped", align_bytes=64)
+            half = D // 2 if c == 0 else 0
+            if half:
+                regroup(nc.vector.tensor_copy, tv_rows[c], tv_grouped, 0, half)
+            regroup(nc.scalar.copy, tv_rows[c], tv_grouped, half, D)
+            regroup(nc.vector.tensor_copy, err_rows[c], err_grouped, half, D)
+            if half:
+                regroup(nc.scalar.copy, err_rows[c], err_grouped, 0, half)
             for j in range(PACK):
                 for m in range(BLOCKS):
                     nc.tensor.matmul(
@@ -113,7 +143,10 @@ def tile_tttinner_pb_t_kernel(tc, err, train_view, test_view, W, b, lr_w, lr_b, 
                         start=(c == 0 and j == 0 and m == 0),
                         stop=(c == CHUNKS - 1 and j == PACK - 1 and m == BLOCKS - 1),
                     )
-            operands[c] = quantise(tv_grouped, "tv") + quantise(err_grouped, "err")
+            return tv_grouped, err_grouped
+
+        def quantise_pair(c, pair):
+            operands[c] = quantise(pair[0], "tv") + quantise(pair[1], "err")
 
         def gradient(c):
             tv_codes, tv_scales, err_codes, err_scales = operands[c]
@@ -130,10 +163,9 @@ def tile_tttinner_pb_t_kernel(tc, err, train_view, test_view, W, b, lr_w, lr_b, 
                 )
 
         b_new = keep.tile([P, BLOCKS], F32)
+        b_spread = keep.tile([P, D], F32)
 
         def update_bias():
-            bias_cols = keep.tile([P, 2 * BLOCKS], F32)
-            nc.vector.tensor_copy(out=bias_cols[:], in_=bias_cols_ps[:, 0 : 2 * BLOCKS])
             bias_step = keep.tile([P, BLOCKS], F32)
             nc.vector.scalar_tensor_tensor(
                 out=bias_step[:],
@@ -145,10 +177,21 @@ def tile_tttinner_pb_t_kernel(tc, err, train_view, test_view, W, b, lr_w, lr_b, 
             )
             nc.vector.tensor_tensor(out=b_new[:], in0=bias_step[:], in1=bias_cols[:, 0:BLOCKS], op=ALU.add)
 
+        def spread_bias():
+            spread = bank(4, [P, D], F32, "spread")
+            for m in range(BLOCKS):
+                nc.tensor.transpose(
+                    out=spread[:, m * P : (m + 1) * P],
+                    in_=b_new[:, m : m + 1].to_broadcast([P, P]),
+                    identity=ident_f32[:],
+                )
+            nc.scalar.copy(out=b_spread[:], in_=spread[:])
+
         q_codes = [keep.tile([P, K_PASS], U32, name="q_codes%d" % g, align_bytes=64) for g in range(CHUNKS)]
         q_scales = [keep.tile([P, K_PASS], U8, name="q_scales%d" % g, align_bytes=64) for g in range(CHUNKS)]
         q_grouped = {}
         zT = {}
+        residual = {}
 
         def q_transpose(g):
             words = q_rows[g][:].bitcast(F32)
@@ -157,7 +200,7 @@ def tile_tttinner_pb_t_kernel(tc, err, train_view, test_view, W, b, lr_w, lr_b, 
             )
             grouped_words = q_grouped[g][:].bitcast(F32).rearrange("p (n u) -> p n u", u=HALVES)
             for h in range(PACK // 2):
-                flipped = plain_psum.tile([P, HALVES, 2 * P], F32, tag="plain")
+                flipped = next_bank("plain", [P, HALVES, 2 * P], F32, "flipped")
                 for jj in range(2):
                     j = 2 * h + jj
                     for u in range(HALVES):
@@ -177,62 +220,108 @@ def tile_tttinner_pb_t_kernel(tc, err, train_view, test_view, W, b, lr_w, lr_b, 
                 out=q_codes[g][:].bitcast(FP8X4), scales=q_scales[g][:], in_=q_grouped[g][:]
             )
 
-        def multiply(g):
-            zT[g] = work.tile([P, BLOCKS, K_PASS], F32, name="zT")
-            for m in range(BLOCKS):
-                o_cols = slice(m * P, (m + 1) * P)
-                product = mx_psum.tile([P, K_PASS], F32, tag="mx")
-                nc.tensor.matmul_mx(
-                    out=product[:],
-                    lhsT=w_codes[:, o_cols].bitcast(FP8X4),
-                    lhsT_scale=w_scales[:, o_cols],
-                    rhs=q_codes[g][:].bitcast(FP8X4),
-                    rhs_scale=q_scales[g][:],
-                    start=True,
-                    stop=True,
-                )
-                nc.scalar.activation(
-                    out=zT[g][:, m, :], in_=product[:], func=ACT.Identity, bias=b_new[:, m : m + 1], scale=1.0
-                )
+        def product(g, m):
+            if m == 0:
+                zT[g] = work.tile([P, BLOCKS, K_PASS], F32, name="zT")
+            o_cols = slice(m * P, (m + 1) * P)
+            result = next_bank("product", [P, K_PASS], F32, "result")
+            nc.tensor.matmul_mx(
+                out=result[:],
+                lhsT=w_codes[:, o_cols].bitcast(FP8X4),
+                lhsT_scale=w_scales[:, o_cols],
+                rhs=q_codes[g][:].bitcast(FP8X4),
+                rhs_scale=q_scales[g][:],
+                start=True,
+                stop=True,
+            )
+            nc.scalar.activation(
+                out=zT[g][:, m, :], in_=result[:], func=ACT.Identity, bias=b_new[:, m : m + 1], scale=1.0
+            )
 
-        def finish(g):
-            z = z_pool.tile([P, PACK, D], F32)
+        def store(g, j, z):
             z_rows = out[g * K_PASS : (g + 1) * K_PASS, :].rearrange("(p j) o -> p j o", j=PACK)
-            for j in range(PACK):
-                back = plain_psum.tile([P, D], F32, tag="plain")
-                for m in range(BLOCKS):
-                    nc.tensor.transpose(
-                        out=back[:, m * P : (m + 1) * P],
-                        in_=zT[g][:, m, j * P : (j + 1) * P],
-                        identity=ident_f32[:],
-                    )
-                nc.vector.tensor_tensor(
-                    out=z[:, j, :], in0=back[:], in1=q_rows[g][:, j * D : (j + 1) * D], op=ALU.add
-                )
-                nc.sync.dma_start(out=z_rows[:, j, :], in_=z[:, j, :])
+            nc.sync.dma_start(out=z_rows[:, j, :], in_=z[:])
 
-        w_new = keep.tile([P, BLOCKS, D], BF16)
+        def finish(g, j):
+            back = next_bank("plain", [P, D], F32, "back")
+            for m in range(BLOCKS):
+                nc.tensor.transpose(
+                    out=back[:, m * P : (m + 1) * P],
+                    in_=zT[g][:, m, j * P : (j + 1) * P],
+                    identity=ident_f32[:],
+                )
+            z = z_pool.tile([P, D], F32, name="z")
+            nc.vector.tensor_tensor(out=z[:], in0=back[:], in1=q_rows[g][:, j * D : (j + 1) * D], op=ALU.add)
+            store(g, j, z)
+
+        def finish_on_scalar(g, j):
+            back = next_bank("plain", [P, D], F32, "back")
+            nc.tensor.matmul(
+                out=back[:], lhsT=ident_bf16[:], rhs=q_rows[g][:, j * D : (j + 1) * D], start=True, stop=False
+            )
+            for m in range(BLOCKS):
+                nc.tensor.matmul(
+                    out=back[:, m * P : (m + 1) * P],
+                    lhsT=zT[g][:, m, j * P : (j + 1) * P],
+                    rhs=ident_f32[:],
+                    is_transpose=True,
+                    start=False,
+                    stop=(m == BLOCKS - 1),
+                )
+            z = z_pool.tile([P, D], F32, name="z")
+            nc.scalar.copy(out=z[:], in_=back[:])
+            store(g, j, z)
+
+        def add_bias(g, j):
+            residual[g, j] = rb_pool.tile([P, D], F32, name="residual")
+            nc.gpsimd.tensor_tensor(
+                out=residual[g, j][:], in0=q_rows[g][:, j * D : (j + 1) * D], in1=b_spread[:], op=ALU.add
+            )
+
+        def direct(g, j):
+            n_cols = slice(j * P, (j + 1) * P)
+            result = next_bank("direct", [P, D], F32, "direct")
+            nc.tensor.matmul_mx(
+                out=result[:],
+                lhsT=q_codes[g][:, n_cols].bitcast(FP8X4),
+                lhsT_scale=q_scales[g][:, n_cols],
+                rhs=w_codes[:].bitcast(FP8X4),
+                rhs_scale=w_scales[:],
+                start=True,
+                stop=True,
+            )
+            z = z_pool.tile([P, D], F32, name="z")
+            nc.vector.tensor_tensor(out=z[:], in0=result[:], in1=residual[g, j][:], op=ALU.add)
+            store(g, j, z)
+
         w_grouped = keep.tile([P, BLOCKS, P, PACK], BF16, align_bytes=64)
         w_codes = keep.tile([P, D], U32, align_bytes=64)
         w_scales = keep.tile([P, D], U8, align_bytes=64)
+        step = {}
 
-        def w_update(m):
-            step = work.tile([P, D], F32, name="step")
+        def w_step(m):
+            step[m] = steps.tile([P, D], F32, name="step")
             nc.vector.scalar_tensor_tensor(
-                out=step[:], in0=grad[m][:], scalar=-COEF, in1=lr_sb[:, m, :], op0=ALU.mult, op1=ALU.mult
+                out=step[m][:], in0=grad[m][:], scalar=-COEF, in1=lr_sb[:, m, :], op0=ALU.mult, op1=ALU.mult
             )
-            nc.vector.tensor_tensor(
-                out=w_new[:, m, :].rearrange("p (u e q) -> p u e q", u=HALVES, e=2),
-                in0=step[:].rearrange("p (u q e) -> p u e q", u=HALVES, e=2),
-                in1=w_sb[:, m, :].rearrange("p (u q e) -> p u e q", u=HALVES, e=2),
-                op=ALU.add,
-            )
-            w_flipped = plain_psum.tile([P, PACK, P], BF16, tag="plain")
-            for t in range(PACK):
-                nc.tensor.transpose(
-                    out=w_flipped[:, t, :], in_=w_new[:, m, t * P : (t + 1) * P], identity=ident_bf16[:]
+
+        def w_sum(m):
+            total = next_bank("plain", [P, PACK, P], F32, "total")
+            runs = [slice(2 * P * u + e, 2 * P * (u + 1), 2) for u in range(HALVES) for e in range(2)]
+            for t, run in enumerate(runs):
+                nc.tensor.matmul(
+                    out=total[:, t, :], lhsT=w_sb[:, m, run], rhs=ident_bf16[:], start=(t == 0), stop=False
                 )
-            nc.scalar.copy(out=w_grouped[:, m], in_=w_flipped[:].rearrange("p t o -> p o t"))
+            for t, run in enumerate(runs):
+                nc.tensor.matmul(
+                    out=total[:, t, :],
+                    lhsT=step[m][:, run],
+                    rhs=ident_f32[:],
+                    is_transpose=True,
+                    start=False,
+                    stop=(t == PACK - 1),
+                )
+            nc.scalar.copy(out=w_grouped[:, m], in_=total[:].rearrange("p t o -> p o t"))
 
         def w_quantise(m):
             o_cols = slice(m * P, (m + 1) * P)
@@ -242,31 +331,70 @@ def tile_tttinner_pb_t_kernel(tc, err, train_view, test_view, W, b, lr_w, lr_b, 
                 in_=w_grouped[:, m].rearrange("p o t -> p (o t)"),
             )
 
-        for c in range(CHUNKS - 1):
+        for c in range(CHUNKS):
+            pair = regroup_pair(c)
+            if c == CHUNKS - 1:
+                update_bias()
+            quantise_pair(c, pair)
+            if c in (2, 4, 6):
+                q_transpose(c // 2 - 1)
+            if c > 0:
+                gradient(c - 1)
             if c == CHUNKS // 2:
-                flip_bias_rows()
-            prepare(c)
-            gradient(c)
-        prepare(CHUNKS - 1)
-        for g in range(AHEAD):
-            q_transpose(g)
+                flipped_bias = flip_bias_rows()
+            if c == CHUNKS // 2 + 1:
+                copy_bias_cols(flipped_bias)
+            if c in (4, 6):
+                q_quantise(c // 2 - 2)
+        spread_bias()
+        direct_slices = [(g, j) for g in DIRECT for j in range(PACK)]
+        for g, j in direct_slices:
+            add_bias(g, j)
+        q_transpose(3)
         gradient(CHUNKS - 1)
-        update_bias()
-
+        q_quantise(2)
+        w_step(0)
+        w_step(1)
+        w_sum(0)
+        w_step(2)
+        w_sum(1)
+        w_quantise(0)
+        w_step(3)
+        w_sum(2)
+        w_quantise(1)
+        w_sum(3)
+        q_quantise(3)
+        w_quantise(2)
+        q_transpose(4)
+        w_quantise(3)
+        for slice_ in direct_slices[:2]:
+            direct(*slice_)
         for m in range(BLOCKS):
-            q_transpose(AHEAD + m)
-            w_update(m)
-            if m > 0:
-                w_quantise(m - 1)
-        for g in range(AHEAD + BLOCKS, CHUNKS):
-            q_transpose(g)
-        q_quantise(0)
-        w_quantise(BLOCKS - 1)
-        for g in range(1, CHUNKS):
-            q_quantise(g)
-
-        multiply(0)
-        for g in range(CHUNKS):
-            if g + 1 < CHUNKS:
-                multiply(g + 1)
-            finish(g)
+            product(0, m)
+        direct(*direct_slices[2])
+        q_quantise(4)
+        direct_slices = direct_slices[3:]
+        for r, g in enumerate(TRANSPOSED):
+            share = SHARES[r]
+            now = direct_slices[:share]
+            direct_slices = direct_slices[share:]
+            if r + 1 < len(TRANSPOSED):
+                for m in range(BLOCKS - 1):
+                    product(TRANSPOSED[r + 1], m)
+                if r > 0:
+                    q_quantise(LATER[r - 1])
+                direct(*now[0])
+                direct(*now[1])
+                product(TRANSPOSED[r + 1], BLOCKS - 1)
+                now = now[2:]
+            else:
+                q_quantise(LATER[r - 1])
+            for j in range(PACK):
+                if j == 3 or (j == 1 and r > 2):
+                    finish_on_scalar(g, j)
+                else:
+                    finish(g, j)
+                if j == 0 and r < 3:
+                    q_transpose(LATER[r])
+            for slice_ in now:
+                direct(*slice_)

@@ -22,11 +22,10 @@ HALVES = 2
 COEF = 2.0 / (TOKENS * D)
 SUM_COLS = 32
 RUN = 4
-EARLY = 3
-TRANSPOSED = (0, 1, 4, 5)
-LATER = (5, 6, 7)
-SHARES = (3, 2, 4, 4)
-DIRECT = (2, 3, 6, 7)
+EARLY = 2
+TRANSPOSED = (0, 1, 2, 3, 4, 5)
+SHARES = (0, 0, 0, 2, 3, 3)
+DIRECT = (6, 7)
 
 FLOPS = 2 * 2 * TOKENS * D * D
 
@@ -41,18 +40,17 @@ def tile_tttinner_pb_t_kernel(tc, err, train_view, test_view, W, b, lr_w, lr_b, 
         work = ctx.enter_context(tc.tile_pool(name="work", bufs=2))
         steps = ctx.enter_context(tc.tile_pool(name="steps", bufs=4))
         z_pool = ctx.enter_context(tc.tile_pool(name="z_pool", bufs=8))
-        rb_pool = ctx.enter_context(tc.tile_pool(name="rb_pool", bufs=16))
+        rb_pool = ctx.enter_context(tc.tile_pool(name="rb_pool", bufs=8))
         banks = ctx.enter_context(tc.psum_pool(name="banks", bufs=1))
-        turn = {"plain": 0, "product": 0, "direct": 0}
-        cycle = {"plain": (6, 7, 5), "product": (0, 1, 2), "direct": (3, 4)}
+        free_banks = [5, 6, 7]
 
         def bank(number, shape, dtype, name):
             return banks.tile(shape, dtype, name=name, tag="bank%d" % number)
 
-        def next_bank(kind, shape, dtype, name):
-            numbers = cycle[kind]
-            number = numbers[turn[kind] % len(numbers)]
-            turn[kind] += 1
+        def next_bank(shape, dtype, name):
+            number = free_banks[0]
+            free_banks.remove(number)
+            free_banks.append(number)
             return bank(number, shape, dtype, name)
 
         def load_rows(source, chunk, name):
@@ -70,13 +68,13 @@ def tile_tttinner_pb_t_kernel(tc, err, train_view, test_view, W, b, lr_w, lr_b, 
         for c in range(CHUNKS):
             tv_rows.append(load_rows(train_view, c, "tv_rows"))
             err_rows.append(load_rows(err, c, "err_rows"))
-            if c in (2, 4, 6, 7):
-                q_rows.append(load_rows(test_view, len(q_rows), "q_rows"))
+        for g in range(EARLY):
+            q_rows.append(load_rows(test_view, g, "q_rows"))
         lr_sb = keep.tile([P, BLOCKS, D], BF16)
         nc.sync.dma_start(out=lr_sb[:], in_=lr_w.rearrange("(m p) i -> p m i", p=P))
         w_sb = keep.tile([P, BLOCKS, D], BF16)
         nc.sync.dma_start(out=w_sb[:], in_=W.rearrange("(m p) i -> p m i", p=P))
-        for g in range(len(q_rows), CHUNKS):
+        for g in range(EARLY, CHUNKS):
             q_rows.append(load_rows(test_view, g, "q_rows"))
 
         ident_f32 = keep.tile([P, P], F32)
@@ -95,7 +93,7 @@ def tile_tttinner_pb_t_kernel(tc, err, train_view, test_view, W, b, lr_w, lr_b, 
         bias_cols = keep.tile([P, 2 * BLOCKS], F32)
 
         def flip_bias_rows():
-            bias_cols_ps = next_bank("plain", [P, P], BF16, "bias_cols_ps")
+            bias_cols_ps = next_bank([P, P], BF16, "bias_cols_ps")
             nc.tensor.transpose(out=bias_cols_ps[:], in_=bias_rows[:], identity=ident_bf16[:])
             return bias_cols_ps
 
@@ -176,9 +174,10 @@ def tile_tttinner_pb_t_kernel(tc, err, train_view, test_view, W, b, lr_w, lr_b, 
                 op1=ALU.mult,
             )
             nc.vector.tensor_tensor(out=b_new[:], in0=bias_step[:], in1=bias_cols[:, 0:BLOCKS], op=ALU.add)
+            free_banks.append(4)
 
         def spread_bias():
-            spread = bank(4, [P, D], F32, "spread")
+            spread = next_bank([P, D], F32, "spread")
             for m in range(BLOCKS):
                 nc.tensor.transpose(
                     out=spread[:, m * P : (m + 1) * P],
@@ -193,14 +192,14 @@ def tile_tttinner_pb_t_kernel(tc, err, train_view, test_view, W, b, lr_w, lr_b, 
         zT = {}
         residual = {}
 
-        def q_transpose(g):
+        def q_transpose(g, copies=(nc.scalar.copy, nc.scalar.copy)):
             words = q_rows[g][:].bitcast(F32)
             q_grouped[g] = keep.tile(
                 [P, PACK * K_PASS], BF16, name="q_grouped%d" % g, tag="tv_rows%d" % g, align_bytes=64
             )
             grouped_words = q_grouped[g][:].bitcast(F32).rearrange("p (n u) -> p n u", u=HALVES)
             for h in range(PACK // 2):
-                flipped = next_bank("plain", [P, HALVES, 2 * P], F32, "flipped")
+                flipped = next_bank([P, HALVES, 2 * P], F32, "flipped")
                 for jj in range(2):
                     j = 2 * h + jj
                     for u in range(HALVES):
@@ -210,7 +209,7 @@ def tile_tttinner_pb_t_kernel(tc, err, train_view, test_view, W, b, lr_w, lr_b, 
                             in_=words[:, first_word : first_word + P],
                             identity=ident_f32[:],
                         )
-                nc.scalar.copy(
+                copies[h](
                     out=grouped_words[:, h * 2 * P : (h + 1) * 2 * P, :],
                     in_=flipped[:].rearrange("p u n -> p n u"),
                 )
@@ -224,7 +223,7 @@ def tile_tttinner_pb_t_kernel(tc, err, train_view, test_view, W, b, lr_w, lr_b, 
             if m == 0:
                 zT[g] = work.tile([P, BLOCKS, K_PASS], F32, name="zT")
             o_cols = slice(m * P, (m + 1) * P)
-            result = next_bank("product", [P, K_PASS], F32, "result")
+            result = next_bank([P, K_PASS], F32, "result")
             nc.tensor.matmul_mx(
                 out=result[:],
                 lhsT=w_codes[:, o_cols].bitcast(FP8X4),
@@ -243,7 +242,7 @@ def tile_tttinner_pb_t_kernel(tc, err, train_view, test_view, W, b, lr_w, lr_b, 
             nc.sync.dma_start(out=z_rows[:, j, :], in_=z[:])
 
         def finish(g, j):
-            back = next_bank("plain", [P, D], F32, "back")
+            back = next_bank([P, D], F32, "back")
             for m in range(BLOCKS):
                 nc.tensor.transpose(
                     out=back[:, m * P : (m + 1) * P],
@@ -255,7 +254,7 @@ def tile_tttinner_pb_t_kernel(tc, err, train_view, test_view, W, b, lr_w, lr_b, 
             store(g, j, z)
 
         def finish_on_scalar(g, j):
-            back = next_bank("plain", [P, D], F32, "back")
+            back = next_bank([P, D], F32, "back")
             nc.tensor.matmul(
                 out=back[:], lhsT=ident_bf16[:], rhs=q_rows[g][:, j * D : (j + 1) * D], start=True, stop=False
             )
@@ -280,7 +279,7 @@ def tile_tttinner_pb_t_kernel(tc, err, train_view, test_view, W, b, lr_w, lr_b, 
 
         def direct(g, j):
             n_cols = slice(j * P, (j + 1) * P)
-            result = next_bank("direct", [P, D], F32, "direct")
+            result = next_bank([P, D], F32, "direct")
             nc.tensor.matmul_mx(
                 out=result[:],
                 lhsT=q_codes[g][:, n_cols].bitcast(FP8X4),
@@ -294,6 +293,7 @@ def tile_tttinner_pb_t_kernel(tc, err, train_view, test_view, W, b, lr_w, lr_b, 
             nc.vector.tensor_tensor(out=z[:], in0=result[:], in1=residual[g, j][:], op=ALU.add)
             store(g, j, z)
 
+        w_new = keep.tile([P, BLOCKS, D], BF16)
         w_grouped = keep.tile([P, BLOCKS, P, PACK], BF16, align_bytes=64)
         w_codes = keep.tile([P, D], U32, align_bytes=64)
         w_scales = keep.tile([P, D], U8, align_bytes=64)
@@ -304,24 +304,23 @@ def tile_tttinner_pb_t_kernel(tc, err, train_view, test_view, W, b, lr_w, lr_b, 
             nc.vector.scalar_tensor_tensor(
                 out=step[m][:], in0=grad[m][:], scalar=-COEF, in1=lr_sb[:, m, :], op0=ALU.mult, op1=ALU.mult
             )
+            free_banks.append(m)
 
-        def w_sum(m):
-            total = next_bank("plain", [P, PACK, P], F32, "total")
-            runs = [slice(2 * P * u + e, 2 * P * (u + 1), 2) for u in range(HALVES) for e in range(2)]
-            for t, run in enumerate(runs):
-                nc.tensor.matmul(
-                    out=total[:, t, :], lhsT=w_sb[:, m, run], rhs=ident_bf16[:], start=(t == 0), stop=False
+        def w_add(m):
+            nc.vector.tensor_tensor(
+                out=w_new[:, m, :].rearrange("p (u e q) -> p u e q", u=HALVES, e=2),
+                in0=step[m][:].rearrange("p (u q e) -> p u e q", u=HALVES, e=2),
+                in1=w_sb[:, m, :].rearrange("p (u q e) -> p u e q", u=HALVES, e=2),
+                op=ALU.add,
+            )
+
+        def w_flip(m):
+            w_flipped = next_bank([P, PACK, P], BF16, "w_flipped")
+            for t in range(PACK):
+                nc.tensor.transpose(
+                    out=w_flipped[:, t, :], in_=w_new[:, m, t * P : (t + 1) * P], identity=ident_bf16[:]
                 )
-            for t, run in enumerate(runs):
-                nc.tensor.matmul(
-                    out=total[:, t, :],
-                    lhsT=step[m][:, run],
-                    rhs=ident_f32[:],
-                    is_transpose=True,
-                    start=False,
-                    stop=(t == PACK - 1),
-                )
-            nc.scalar.copy(out=w_grouped[:, m], in_=total[:].rearrange("p t o -> p o t"))
+            nc.scalar.copy(out=w_grouped[:, m], in_=w_flipped[:].rearrange("p t o -> p o t"))
 
         def w_quantise(m):
             o_cols = slice(m * P, (m + 1) * P)
@@ -335,66 +334,65 @@ def tile_tttinner_pb_t_kernel(tc, err, train_view, test_view, W, b, lr_w, lr_b, 
             pair = regroup_pair(c)
             if c == CHUNKS - 1:
                 update_bias()
+                q_transpose(0)
             quantise_pair(c, pair)
-            if c in (2, 4, 6):
-                q_transpose(c // 2 - 1)
             if c > 0:
                 gradient(c - 1)
             if c == CHUNKS // 2:
                 flipped_bias = flip_bias_rows()
             if c == CHUNKS // 2 + 1:
                 copy_bias_cols(flipped_bias)
-            if c in (4, 6):
-                q_quantise(c // 2 - 2)
-        spread_bias()
-        direct_slices = [(g, j) for g in DIRECT for j in range(PACK)]
-        for g, j in direct_slices:
-            add_bias(g, j)
-        q_transpose(3)
+        q_transpose(1)
         gradient(CHUNKS - 1)
-        q_quantise(2)
+        q_quantise(0)
+        q_transpose(2)
         w_step(0)
         w_step(1)
-        w_sum(0)
+        w_add(0)
+        w_flip(0)
         w_step(2)
-        w_sum(1)
-        w_quantise(0)
+        w_add(1)
+        w_flip(1)
+        q_transpose(3)
         w_step(3)
-        w_sum(2)
+        w_add(2)
+        w_flip(2)
+        w_quantise(0)
+        w_add(3)
+        w_flip(3)
         w_quantise(1)
-        w_sum(3)
-        q_quantise(3)
+        q_quantise(1)
         w_quantise(2)
         q_transpose(4)
         w_quantise(3)
-        for slice_ in direct_slices[:2]:
-            direct(*slice_)
+        q_quantise(2)
         for m in range(BLOCKS):
             product(0, m)
-        direct(*direct_slices[2])
+        q_quantise(3)
+        q_transpose(5, (nc.vector.tensor_copy, nc.vector.tensor_copy))
         q_quantise(4)
-        direct_slices = direct_slices[3:]
+        direct_slices = [(g, j) for g in DIRECT for j in range(PACK)]
         for r, g in enumerate(TRANSPOSED):
-            share = SHARES[r]
-            now = direct_slices[:share]
-            direct_slices = direct_slices[share:]
-            if r + 1 < len(TRANSPOSED):
+            now = direct_slices[: SHARES[r]]
+            direct_slices = direct_slices[SHARES[r] :]
+            last = r + 1 == len(TRANSPOSED)
+            if not last:
                 for m in range(BLOCKS - 1):
                     product(TRANSPOSED[r + 1], m)
-                if r > 0:
-                    q_quantise(LATER[r - 1])
-                direct(*now[0])
-                direct(*now[1])
+            if r < 3:
+                q_quantise(5 + r)
+            for slice_ in now:
+                direct(*slice_)
+            if not last:
                 product(TRANSPOSED[r + 1], BLOCKS - 1)
-                now = now[2:]
-            else:
-                q_quantise(LATER[r - 1])
             for j in range(PACK):
-                if j == 3 or (j == 1 and r > 2):
+                if r > 3 and j % 2 == 1:
                     finish_on_scalar(g, j)
                 else:
                     finish(g, j)
-                if j == 0 and r < 3:
-                    q_transpose(LATER[r])
-            for slice_ in now:
-                direct(*slice_)
+                if j == 1 and r < 2:
+                    q_transpose(6 + r)
+            if r == 1:
+                spread_bias()
+                for slice_ in direct_slices:
+                    add_bias(*slice_)

@@ -22,7 +22,7 @@ HALVES = 2
 COEF = 2.0 / (TOKENS * D)
 SUM_COLS = 32
 RUN = 4
-EARLY = 2
+EARLY = 3
 TRANSPOSED = (0, 1, 2, 3, 4, 5)
 SHARES = (0, 0, 0, 2, 3, 3)
 DIRECT = (6, 7)
@@ -126,12 +126,13 @@ def tile_tttinner_pb_t_kernel(tc, err, train_view, test_view, W, b, lr_w, lr_b, 
             tv_grouped = grouped.tile([P, D, PACK], BF16, name="tv_grouped", align_bytes=64)
             err_grouped = grouped.tile([P, D, PACK], BF16, name="err_grouped", align_bytes=64)
             half = D // 2 if c == 0 else 0
+            tail_half = D // 2 if c == CHUNKS - 1 else 0
             if half:
                 regroup(nc.vector.tensor_copy, tv_rows[c], tv_grouped, 0, half)
             regroup(nc.scalar.copy, tv_rows[c], tv_grouped, half, D)
-            regroup(nc.vector.tensor_copy, err_rows[c], err_grouped, half, D)
-            if half:
-                regroup(nc.scalar.copy, err_rows[c], err_grouped, 0, half)
+            regroup(nc.vector.tensor_copy, err_rows[c], err_grouped, half + tail_half, D)
+            if half + tail_half:
+                regroup(nc.scalar.copy, err_rows[c], err_grouped, 0, half + tail_half)
             for j in range(PACK):
                 for m in range(BLOCKS):
                     nc.tensor.matmul(
@@ -293,7 +294,6 @@ def tile_tttinner_pb_t_kernel(tc, err, train_view, test_view, W, b, lr_w, lr_b, 
             nc.vector.tensor_tensor(out=z[:], in0=result[:], in1=residual[g, j][:], op=ALU.add)
             store(g, j, z)
 
-        w_new = keep.tile([P, BLOCKS, D], BF16)
         w_grouped = keep.tile([P, BLOCKS, P, PACK], BF16, align_bytes=64)
         w_codes = keep.tile([P, D], U32, align_bytes=64)
         w_scales = keep.tile([P, D], U8, align_bytes=64)
@@ -306,21 +306,23 @@ def tile_tttinner_pb_t_kernel(tc, err, train_view, test_view, W, b, lr_w, lr_b, 
             )
             free_banks.append(m)
 
-        def w_add(m):
-            nc.vector.tensor_tensor(
-                out=w_new[:, m, :].rearrange("p (u e q) -> p u e q", u=HALVES, e=2),
-                in0=step[m][:].rearrange("p (u q e) -> p u e q", u=HALVES, e=2),
-                in1=w_sb[:, m, :].rearrange("p (u q e) -> p u e q", u=HALVES, e=2),
-                op=ALU.add,
-            )
-
-        def w_flip(m):
-            w_flipped = next_bank([P, PACK, P], BF16, "w_flipped")
-            for t in range(PACK):
-                nc.tensor.transpose(
-                    out=w_flipped[:, t, :], in_=w_new[:, m, t * P : (t + 1) * P], identity=ident_bf16[:]
+        def w_sum(m):
+            total = next_bank([P, PACK, P], F32, "total")
+            runs = [slice(2 * P * u + e, 2 * P * (u + 1), 2) for u in range(HALVES) for e in range(2)]
+            for t, run in enumerate(runs):
+                nc.tensor.matmul(
+                    out=total[:, t, :], lhsT=w_sb[:, m, run], rhs=ident_bf16[:], start=(t == 0), stop=False
                 )
-            nc.scalar.copy(out=w_grouped[:, m], in_=w_flipped[:].rearrange("p t o -> p o t"))
+            for t, run in enumerate(runs):
+                nc.tensor.matmul(
+                    out=total[:, t, :],
+                    lhsT=step[m][:, run],
+                    rhs=ident_f32[:],
+                    is_transpose=True,
+                    start=False,
+                    stop=(t == PACK - 1),
+                )
+            nc.scalar.copy(out=w_grouped[:, m], in_=total[:].rearrange("p t o -> p o t"))
 
         def w_quantise(m):
             o_cols = slice(m * P, (m + 1) * P)
@@ -343,31 +345,27 @@ def tile_tttinner_pb_t_kernel(tc, err, train_view, test_view, W, b, lr_w, lr_b, 
             if c == CHUNKS // 2 + 1:
                 copy_bias_cols(flipped_bias)
         q_transpose(1)
+        q_transpose(2)
         gradient(CHUNKS - 1)
         q_quantise(0)
-        q_transpose(2)
         w_step(0)
         w_step(1)
-        w_add(0)
-        w_flip(0)
+        w_sum(0)
         w_step(2)
-        w_add(1)
-        w_flip(1)
-        q_transpose(3)
+        w_sum(1)
         w_step(3)
-        w_add(2)
-        w_flip(2)
         w_quantise(0)
-        w_add(3)
-        w_flip(3)
+        w_sum(2)
         w_quantise(1)
+        w_sum(3)
         q_quantise(1)
         w_quantise(2)
-        q_transpose(4)
+        q_transpose(3, (nc.vector.tensor_copy, nc.scalar.copy))
         w_quantise(3)
         q_quantise(2)
         for m in range(BLOCKS):
             product(0, m)
+        q_transpose(4, (nc.vector.tensor_copy, nc.scalar.copy))
         q_quantise(3)
         q_transpose(5, (nc.vector.tensor_copy, nc.vector.tensor_copy))
         q_quantise(4)

@@ -23,9 +23,9 @@ COEF = 2.0 / (TOKENS * D)
 SUM_COLS = 32
 RUN = 4
 EARLY = 3
-TRANSPOSED = (0, 1, 2, 3, 4, 5)
-SHARES = (0, 0, 0, 2, 3, 3)
-DIRECT = (6, 7)
+TRANSPOSED = (0, 1, 2, 3, 4)
+SHARES = (0, 1, 3, 4, 4)
+DIRECT = (5, 6, 7)
 
 FLOPS = 2 * 2 * TOKENS * D * D
 
@@ -40,7 +40,6 @@ def tile_tttinner_pb_t_kernel(tc, err, train_view, test_view, W, b, lr_w, lr_b, 
         work = ctx.enter_context(tc.tile_pool(name="work", bufs=2))
         steps = ctx.enter_context(tc.tile_pool(name="steps", bufs=4))
         z_pool = ctx.enter_context(tc.tile_pool(name="z_pool", bufs=8))
-        rb_pool = ctx.enter_context(tc.tile_pool(name="rb_pool", bufs=8))
         banks = ctx.enter_context(tc.psum_pool(name="banks", bufs=1))
         free_banks = [5, 6, 7]
 
@@ -272,11 +271,16 @@ def tile_tttinner_pb_t_kernel(tc, err, train_view, test_view, W, b, lr_w, lr_b, 
             nc.scalar.copy(out=z[:], in_=back[:])
             store(g, j, z)
 
-        def add_bias(g, j):
-            residual[g, j] = rb_pool.tile([P, D], F32, name="residual")
-            nc.gpsimd.tensor_tensor(
-                out=residual[g, j][:], in0=q_rows[g][:, j * D : (j + 1) * D], in1=b_spread[:], op=ALU.add
+        def add_bias(g, h, bytes_of):
+            pair = keep.tile(
+                [P, 2, D], F32, name="residual%d" % bytes_of, tag="tv_rows%d" % bytes_of, align_bytes=64
             )
+            for i in range(2):
+                j = 2 * h + i
+                residual[g, j] = pair[:, i, :]
+                nc.gpsimd.tensor_tensor(
+                    out=pair[:, i, :], in0=q_rows[g][:, j * D : (j + 1) * D], in1=b_spread[:], op=ALU.add
+                )
 
         def direct(g, j):
             n_cols = slice(j * P, (j + 1) * P)
@@ -291,7 +295,7 @@ def tile_tttinner_pb_t_kernel(tc, err, train_view, test_view, W, b, lr_w, lr_b, 
                 stop=True,
             )
             z = z_pool.tile([P, D], F32, name="z")
-            nc.vector.tensor_tensor(out=z[:], in0=result[:], in1=residual[g, j][:], op=ALU.add)
+            nc.vector.tensor_tensor(out=z[:], in0=result[:], in1=residual[g, j], op=ALU.add)
             store(g, j, z)
 
         w_grouped = keep.tile([P, BLOCKS, P, PACK], BF16, align_bytes=64)
@@ -301,9 +305,16 @@ def tile_tttinner_pb_t_kernel(tc, err, train_view, test_view, W, b, lr_w, lr_b, 
 
         def w_step(m):
             step[m] = steps.tile([P, D], F32, name="step")
-            nc.vector.scalar_tensor_tensor(
-                out=step[m][:], in0=grad[m][:], scalar=-COEF, in1=lr_sb[:, m, :], op0=ALU.mult, op1=ALU.mult
-            )
+            for u in range(HALVES):
+                half = slice(2 * P * u, 2 * P * (u + 1))
+                nc.vector.scalar_tensor_tensor(
+                    out=step[m][:, half].rearrange("p (e q) -> p e q", e=2),
+                    in0=grad[m][:, half].rearrange("p (q e) -> p e q", e=2),
+                    scalar=-COEF,
+                    in1=lr_sb[:, m, half].rearrange("p (q e) -> p e q", e=2),
+                    op0=ALU.mult,
+                    op1=ALU.mult,
+                )
             free_banks.append(m)
 
         def w_sum(m):
@@ -316,7 +327,7 @@ def tile_tttinner_pb_t_kernel(tc, err, train_view, test_view, W, b, lr_w, lr_b, 
             for t, run in enumerate(runs):
                 nc.tensor.matmul(
                     out=total[:, t, :],
-                    lhsT=step[m][:, run],
+                    lhsT=step[m][:, t * P : (t + 1) * P],
                     rhs=ident_f32[:],
                     is_transpose=True,
                     start=False,
@@ -356,6 +367,7 @@ def tile_tttinner_pb_t_kernel(tc, err, train_view, test_view, W, b, lr_w, lr_b, 
         w_step(3)
         w_quantise(0)
         w_sum(2)
+        spread_bias()
         w_quantise(1)
         w_sum(3)
         q_quantise(1)
@@ -363,10 +375,12 @@ def tile_tttinner_pb_t_kernel(tc, err, train_view, test_view, W, b, lr_w, lr_b, 
         q_transpose(3, (nc.vector.tensor_copy, nc.scalar.copy))
         w_quantise(3)
         q_quantise(2)
-        for m in range(BLOCKS):
-            product(0, m)
         q_transpose(4, (nc.vector.tensor_copy, nc.scalar.copy))
+        product(0, 0)
+        product(0, 1)
         q_quantise(3)
+        product(0, 2)
+        product(0, 3)
         q_transpose(5, (nc.vector.tensor_copy, nc.vector.tensor_copy))
         q_quantise(4)
         direct_slices = [(g, j) for g in DIRECT for j in range(PACK)]
@@ -379,18 +393,19 @@ def tile_tttinner_pb_t_kernel(tc, err, train_view, test_view, W, b, lr_w, lr_b, 
                     product(TRANSPOSED[r + 1], m)
             if r < 3:
                 q_quantise(5 + r)
+            if r < 2:
+                add_bias(5, r, 5 + r)
+            if r == 2:
+                for i in range(4):
+                    add_bias(6 + i // 2, i % 2, 7 - i if i == 0 else 5 - i)
             for slice_ in now:
                 direct(*slice_)
             if not last:
                 product(TRANSPOSED[r + 1], BLOCKS - 1)
             for j in range(PACK):
-                if r > 3 and j % 2 == 1:
+                if r > 0 and j == 3 or r > 2 and j == 1:
                     finish_on_scalar(g, j)
                 else:
                     finish(g, j)
                 if j == 1 and r < 2:
                     q_transpose(6 + r)
-            if r == 1:
-                spread_bias()
-                for slice_ in direct_slices:
-                    add_bias(*slice_)

@@ -24,7 +24,7 @@ SUM_COLS = 32
 RUN = 4
 EARLY = 3
 TRANSPOSED = (0, 1, 2, 3, 4)
-SHARES = (0, 1, 3, 4, 4)
+SHARES = (0, 2, 2, 4, 4)
 DIRECT = (5, 6, 7)
 
 FLOPS = 2 * 2 * TOKENS * D * D
@@ -39,7 +39,7 @@ def tile_tttinner_pb_t_kernel(tc, err, train_view, test_view, W, b, lr_w, lr_b, 
         packed = ctx.enter_context(tc.tile_pool(name="packed", bufs=3))
         work = ctx.enter_context(tc.tile_pool(name="work", bufs=2))
         steps = ctx.enter_context(tc.tile_pool(name="steps", bufs=4))
-        z_pool = ctx.enter_context(tc.tile_pool(name="z_pool", bufs=8))
+        z_pool = ctx.enter_context(tc.tile_pool(name="z_pool", bufs=6))
         banks = ctx.enter_context(tc.psum_pool(name="banks", bufs=1))
         free_banks = [5, 6, 7]
 
@@ -237,9 +237,20 @@ def tile_tttinner_pb_t_kernel(tc, err, train_view, test_view, W, b, lr_w, lr_b, 
                 out=zT[g][:, m, :], in_=result[:], func=ACT.Identity, bias=b_new[:, m : m + 1], scale=1.0
             )
 
-        def store(g, j, z):
+        z_pairs = {}
+
+        def z_slice(g, j):
+            if j % 2 == 0:
+                z_pairs[g, j // 2] = z_pool.tile([P, 2, D], F32, name="z")
+            return z_pairs[g, j // 2][:, j % 2, :]
+
+        def store(g, j):
             z_rows = out[g * K_PASS : (g + 1) * K_PASS, :].rearrange("(p j) o -> p j o", j=PACK)
-            nc.sync.dma_start(out=z_rows[:, j, :], in_=z[:])
+            pair = z_pairs[g, j // 2]
+            if g == DIRECT[-1] and j >= PACK // 2:
+                nc.sync.dma_start(out=z_rows[:, j, :], in_=pair[:, j % 2, :])
+            elif j % 2 == 1:
+                nc.sync.dma_start(out=z_rows[:, j - 1 : j + 1, :], in_=pair[:])
 
         def finish(g, j):
             back = next_bank([P, D], F32, "back")
@@ -249,9 +260,9 @@ def tile_tttinner_pb_t_kernel(tc, err, train_view, test_view, W, b, lr_w, lr_b, 
                     in_=zT[g][:, m, j * P : (j + 1) * P],
                     identity=ident_f32[:],
                 )
-            z = z_pool.tile([P, D], F32, name="z")
-            nc.vector.tensor_tensor(out=z[:], in0=back[:], in1=q_rows[g][:, j * D : (j + 1) * D], op=ALU.add)
-            store(g, j, z)
+            z = z_slice(g, j)
+            nc.vector.tensor_tensor(out=z, in0=back[:], in1=q_rows[g][:, j * D : (j + 1) * D], op=ALU.add)
+            store(g, j)
 
         def finish_on_scalar(g, j):
             back = next_bank([P, D], F32, "back")
@@ -267,9 +278,9 @@ def tile_tttinner_pb_t_kernel(tc, err, train_view, test_view, W, b, lr_w, lr_b, 
                     start=False,
                     stop=(m == BLOCKS - 1),
                 )
-            z = z_pool.tile([P, D], F32, name="z")
-            nc.scalar.copy(out=z[:], in_=back[:])
-            store(g, j, z)
+            z = z_slice(g, j)
+            nc.scalar.copy(out=z, in_=back[:])
+            store(g, j)
 
         def add_bias(g, h, bytes_of):
             pair = keep.tile(
@@ -294,9 +305,9 @@ def tile_tttinner_pb_t_kernel(tc, err, train_view, test_view, W, b, lr_w, lr_b, 
                 start=True,
                 stop=True,
             )
-            z = z_pool.tile([P, D], F32, name="z")
-            nc.vector.tensor_tensor(out=z[:], in0=result[:], in1=residual[g, j], op=ALU.add)
-            store(g, j, z)
+            z = z_slice(g, j)
+            nc.vector.tensor_tensor(out=z, in0=result[:], in1=residual[g, j], op=ALU.add)
+            store(g, j)
 
         w_grouped = keep.tile([P, BLOCKS, P, PACK], BF16, align_bytes=64)
         w_codes = keep.tile([P, D], U32, align_bytes=64)

@@ -70,9 +70,10 @@ def tile_tttinner_pb_t_kernel(tc, err, train_view, test_view, W, b, lr_w, lr_b, 
         for g in range(EARLY):
             q_rows.append(load_rows(test_view, g, "q_rows"))
         lr_sb = keep.tile([P, BLOCKS, D], BF16)
-        nc.sync.dma_start(out=lr_sb[:], in_=lr_w.rearrange("(m p) i -> p m i", p=P))
         w_sb = keep.tile([P, BLOCKS, D], BF16)
-        nc.sync.dma_start(out=w_sb[:], in_=W.rearrange("(m p) i -> p m i", p=P))
+        for m in range(BLOCKS):
+            nc.sync.dma_start(out=lr_sb[:, m, :], in_=lr_w[m * P : (m + 1) * P, :])
+            nc.sync.dma_start(out=w_sb[:, m, :], in_=W[m * P : (m + 1) * P, :])
         for g in range(EARLY, CHUNKS):
             q_rows.append(load_rows(test_view, g, "q_rows"))
 

from contextlib import ExitStack

import concourse.mybir as mybir
from concourse.masks import make_identity

F32 = mybir.dt.float32
BF16 = mybir.dt.bfloat16
U32 = mybir.dt.uint32
U8 = mybir.dt.uint8
FP8X4 = mybir.dt.float8_e4m3fn_x4
ALU = mybir.AluOpType
ACT = mybir.ActivationFunctionType

P = 128
PACK = 4
K_PASS = P * PACK
TOKENS = 4096
D = 512
CHUNKS = TOKENS // K_PASS
BLOCKS = D // P
HALVES = 2
COEF = 2.0 / (TOKENS * D)
SUM_COLS = 32
RUN = 4
EARLY = 3
TRANSPOSED = (0, 1, 2, 3, 4)
SHARES = (0, 2, 2, 4, 4)
DIRECT = (5, 6, 7)

FLOPS = 2 * 2 * TOKENS * D * D


def tile_tttinner_pb_t_kernel(tc, err, train_view, test_view, W, b, lr_w, lr_b, out):
    nc = tc.nc
    with ExitStack() as ctx:
        ctx.enter_context(tc.manual_schedule())
        keep = ctx.enter_context(tc.tile_pool(name="keep", bufs=1))
        grouped = ctx.enter_context(tc.tile_pool(name="grouped", bufs=2))
        packed = ctx.enter_context(tc.tile_pool(name="packed", bufs=3))
        work = ctx.enter_context(tc.tile_pool(name="work", bufs=2))
        steps = ctx.enter_context(tc.tile_pool(name="steps", bufs=4))
        z_pool = ctx.enter_context(tc.tile_pool(name="z_pool", bufs=6))
        banks = ctx.enter_context(tc.psum_pool(name="banks", bufs=1))
        free_banks = [5, 6, 7]

        def bank(number, shape, dtype, name):
            return banks.tile(shape, dtype, name=name, tag="bank%d" % number)

        def next_bank(shape, dtype, name):
            number = free_banks[0]
            free_banks.remove(number)
            free_banks.append(number)
            return bank(number, shape, dtype, name)

        def load_rows(source, chunk, name):
            label = "%s%d" % (name, chunk)
            rows = keep.tile([P, PACK * D], BF16, name=label, tag=label, align_bytes=64)
            nc.sync.dma_start(
                out=rows[:].rearrange("p (j w) -> p j w", j=PACK),
                in_=source[chunk * K_PASS : (chunk + 1) * K_PASS, :].rearrange("(p j) w -> p j w", j=PACK),
            )
            return rows

        tv_rows = []
        err_rows = []
        q_rows = []
        for c in range(CHUNKS):
            tv_rows.append(load_rows(train_view, c, "tv_rows"))
            err_rows.append(load_rows(err, c, "err_rows"))
        for g in range(EARLY):
            q_rows.append(load_rows(test_view, g, "q_rows"))
        lr_sb = keep.tile([P, BLOCKS, D], BF16)
        w_sb = keep.tile([P, BLOCKS, D], BF16)
        for m in range(BLOCKS):
            nc.sync.dma_start(out=lr_sb[:, m, :], in_=lr_w[m * P : (m + 1) * P, :])
            nc.sync.dma_start(out=w_sb[:, m, :], in_=W[m * P : (m + 1) * P, :])
        for g in range(EARLY, CHUNKS):
            q_rows.append(load_rows(test_view, g, "q_rows"))

        ident_f32 = keep.tile([P, P], F32)
        make_identity(nc, ident_f32[:])
        ident_bf16 = keep.tile([P, P], BF16)
        make_identity(nc, ident_bf16[:])
        ones = keep.tile([P, SUM_COLS], BF16)
        nc.vector.memset(ones[:], 1.0)
        table_warmer = keep.tile([P, 1], F32)
        nc.scalar.activation(out=table_warmer[:], in_=ones[:, 0:1], func=ACT.Identity)

        bias_rows = keep.tile([P, P], BF16)
        nc.vector.memset(bias_rows[:], 0.0)
        nc.scalar.dma_start(out=bias_rows[0:BLOCKS, :], in_=b.rearrange("(m p) -> m p", p=P))
        nc.scalar.dma_start(out=bias_rows[BLOCKS : 2 * BLOCKS, :], in_=lr_b.rearrange("(m p) -> m p", p=P))
        bias_cols = keep.tile([P, 2 * BLOCKS], F32)

        def flip_bias_rows():
            bias_cols_ps = next_bank([P, P], BF16, "bias_cols_ps")
            nc.tensor.transpose(out=bias_cols_ps[:], in_=bias_rows[:], identity=ident_bf16[:])
            return bias_cols_ps

        def copy_bias_cols(bias_cols_ps):
            nc.vector.tensor_copy(out=bias_cols[:], in_=bias_cols_ps[:, 0 : 2 * BLOCKS])

        grad = [bank(m, [P, D], F32, "grad%d" % m) for m in range(BLOCKS)]
        err_sum = bank(4, [P, BLOCKS, SUM_COLS], F32, "err_sum")
        operands = {}

        def regroup(engine_copy, rows, side_by_side, first, last):
            engine_copy(
                out=side_by_side[:, first:last, :].rearrange("p (c i) j -> p c j i", i=RUN),
                in_=rows[:].rearrange("p (j w) -> p j w", j=PACK)[:, :, first:last].rearrange(
                    "p j (c i) -> p c j i", i=RUN
                ),
            )

        def quantise(side_by_side, name):
            codes = packed.tile([P, D], U32, name=name + "_codes", align_bytes=64)
            scales = packed.tile([P, D], U8, name=name + "_scales", align_bytes=64)
            nc.vector.quantize_mx(
                out=codes[:].bitcast(FP8X4),
                scales=scales[:],
                in_=side_by_side[:].rearrange("p w j -> p (w j)"),
            )
            return codes, scales

        def regroup_pair(c):
            tv_grouped = grouped.tile([P, D, PACK], BF16, name="tv_grouped", align_bytes=64)
            err_grouped = grouped.tile([P, D, PACK], BF16, name="err_grouped", align_bytes=64)
            half = D // 2 if c == 0 else 0
            tail_half = D // 2 if c == CHUNKS - 1 else 0
            if half:
                regroup(nc.vector.tensor_copy, tv_rows[c], tv_grouped, 0, half)
            regroup(nc.scalar.copy, tv_rows[c], tv_grouped, half, D)
            regroup(nc.vector.tensor_copy, err_rows[c], err_grouped, half + tail_half, D)
            if half + tail_half:
                regroup(nc.scalar.copy, err_rows[c], err_grouped, 0, half + tail_half)
            for j in range(PACK):
                for m in range(BLOCKS):
                    nc.tensor.matmul(
                        out=err_sum[:, m, :],
                        lhsT=err_rows[c][:, j * D + m * P : j * D + (m + 1) * P],
                        rhs=ones[:],
                        start=(c == 0 and j == 0 and m == 0),
                        stop=(c == CHUNKS - 1 and j == PACK - 1 and m == BLOCKS - 1),
                    )
            return tv_grouped, err_grouped

        def quantise_pair(c, pair):
            operands[c] = quantise(pair[0], "tv") + quantise(pair[1], "err")

        def gradient(c):
            tv_codes, tv_scales, err_codes, err_scales = operands[c]
            for m in range(BLOCKS):
                o_cols = slice(m * P, (m + 1) * P)
                nc.tensor.matmul_mx(
                    out=grad[m][:],
                    lhsT=err_codes[:, o_cols].bitcast(FP8X4),
                    lhsT_scale=err_scales[:, o_cols],
                    rhs=tv_codes[:].bitcast(FP8X4),
                    rhs_scale=tv_scales[:],
                    start=(c == 0),
                    stop=(c == CHUNKS - 1),
                )

        b_new = keep.tile([P, BLOCKS], F32)
        b_spread = keep.tile([P, D], F32)

        def update_bias():
            bias_step = keep.tile([P, BLOCKS], F32)
            nc.vector.scalar_tensor_tensor(
                out=bias_step[:],
                in0=err_sum[:, :, 0],
                scalar=-COEF,
                in1=bias_cols[:, BLOCKS : 2 * BLOCKS],
                op0=ALU.mult,
                op1=ALU.mult,
            )
            nc.vector.tensor_tensor(out=b_new[:], in0=bias_step[:], in1=bias_cols[:, 0:BLOCKS], op=ALU.add)
            free_banks.append(4)

        def spread_bias():
            spread = next_bank([P, D], F32, "spread")
            for m in range(BLOCKS):
                nc.tensor.transpose(
                    out=spread[:, m * P : (m + 1) * P],
                    in_=b_new[:, m : m + 1].to_broadcast([P, P]),
                    identity=ident_f32[:],
                )
            nc.scalar.copy(out=b_spread[:], in_=spread[:])

        q_codes = [keep.tile([P, K_PASS], U32, name="q_codes%d" % g, align_bytes=64) for g in range(CHUNKS)]
        q_scales = [keep.tile([P, K_PASS], U8, name="q_scales%d" % g, align_bytes=64) for g in range(CHUNKS)]
        q_grouped = {}
        zT = {}
        residual = {}

        def q_transpose(g, copies=(nc.scalar.copy, nc.scalar.copy)):
            words = q_rows[g][:].bitcast(F32)
            q_grouped[g] = keep.tile(
                [P, PACK * K_PASS], BF16, name="q_grouped%d" % g, tag="tv_rows%d" % g, align_bytes=64
            )
            grouped_words = q_grouped[g][:].bitcast(F32).rearrange("p (n u) -> p n u", u=HALVES)
            for h in range(PACK // 2):
                flipped = next_bank([P, HALVES, 2 * P], F32, "flipped")
                for jj in range(2):
                    j = 2 * h + jj
                    for u in range(HALVES):
                        first_word = (j * HALVES + u) * P
                        nc.tensor.transpose(
                            out=flipped[:, u, jj * P : (jj + 1) * P],
                            in_=words[:, first_word : first_word + P],
                            identity=ident_f32[:],
                        )
                copies[h](
                    out=grouped_words[:, h * 2 * P : (h + 1) * 2 * P, :],
                    in_=flipped[:].rearrange("p u n -> p n u"),
                )

        def q_quantise(g):
            nc.vector.quantize_mx(
                out=q_codes[g][:].bitcast(FP8X4), scales=q_scales[g][:], in_=q_grouped[g][:]
            )

        def product(g, m):
            if m == 0:
                zT[g] = work.tile([P, BLOCKS, K_PASS], F32, name="zT")
            o_cols = slice(m * P, (m + 1) * P)
            result = next_bank([P, K_PASS], F32, "result")
            nc.tensor.matmul_mx(
                out=result[:],
                lhsT=w_codes[:, o_cols].bitcast(FP8X4),
                lhsT_scale=w_scales[:, o_cols],
                rhs=q_codes[g][:].bitcast(FP8X4),
                rhs_scale=q_scales[g][:],
                start=True,
                stop=True,
            )
            nc.scalar.activation(
                out=zT[g][:, m, :], in_=result[:], func=ACT.Identity, bias=b_new[:, m : m + 1], scale=1.0
            )

        z_pairs = {}

        def z_slice(g, j):
            if j % 2 == 0:
                z_pairs[g, j // 2] = z_pool.tile([P, 2, D], F32, name="z")
            return z_pairs[g, j // 2][:, j % 2, :]

        def store(g, j):
            z_rows = out[g * K_PASS : (g + 1) * K_PASS, :].rearrange("(p j) o -> p j o", j=PACK)
            pair = z_pairs[g, j // 2]
            if g == DIRECT[-1] and j >= PACK // 2:
                nc.sync.dma_start(out=z_rows[:, j, :], in_=pair[:, j % 2, :])
            elif j % 2 == 1:
                nc.sync.dma_start(out=z_rows[:, j - 1 : j + 1, :], in_=pair[:])

        def finish(g, j):
            back = next_bank([P, D], F32, "back")
            for m in range(BLOCKS):
                nc.tensor.transpose(
                    out=back[:, m * P : (m + 1) * P],
                    in_=zT[g][:, m, j * P : (j + 1) * P],
                    identity=ident_f32[:],
                )
            z = z_slice(g, j)
            nc.vector.tensor_tensor(out=z, in0=back[:], in1=q_rows[g][:, j * D : (j + 1) * D], op=ALU.add)
            store(g, j)

        def finish_on_scalar(g, j):
            back = next_bank([P, D], F32, "back")
            nc.tensor.matmul(
                out=back[:], lhsT=ident_bf16[:], rhs=q_rows[g][:, j * D : (j + 1) * D], start=True, stop=False
            )
            for m in range(BLOCKS):
                nc.tensor.matmul(
                    out=back[:, m * P : (m + 1) * P],
                    lhsT=zT[g][:, m, j * P : (j + 1) * P],
                    rhs=ident_f32[:],
                    is_transpose=True,
                    start=False,
                    stop=(m == BLOCKS - 1),
                )
            z = z_slice(g, j)
            nc.scalar.copy(out=z, in_=back[:])
            store(g, j)

        def add_bias(g, h, bytes_of):
            pair = keep.tile(
                [P, 2, D], F32, name="residual%d" % bytes_of, tag="tv_rows%d" % bytes_of, align_bytes=64
            )
            for i in range(2):
                j = 2 * h + i
                residual[g, j] = pair[:, i, :]
                nc.gpsimd.tensor_tensor(
                    out=pair[:, i, :], in0=q_rows[g][:, j * D : (j + 1) * D], in1=b_spread[:], op=ALU.add
                )

        def direct(g, j):
            n_cols = slice(j * P, (j + 1) * P)
            result = next_bank([P, D], F32, "direct")
            nc.tensor.matmul_mx(
                out=result[:],
                lhsT=q_codes[g][:, n_cols].bitcast(FP8X4),
                lhsT_scale=q_scales[g][:, n_cols],
                rhs=w_codes[:].bitcast(FP8X4),
                rhs_scale=w_scales[:],
                start=True,
                stop=True,
            )
            z = z_slice(g, j)
            nc.vector.tensor_tensor(out=z, in0=result[:], in1=residual[g, j], op=ALU.add)
            store(g, j)

        w_grouped = keep.tile([P, BLOCKS, P, PACK], BF16, align_bytes=64)
        w_codes = keep.tile([P, D], U32, align_bytes=64)
        w_scales = keep.tile([P, D], U8, align_bytes=64)
        step = {}

        def w_step(m):
            step[m] = steps.tile([P, D], F32, name="step")
            for u in range(HALVES):
                half = slice(2 * P * u, 2 * P * (u + 1))
                nc.vector.scalar_tensor_tensor(
                    out=step[m][:, half].rearrange("p (e q) -> p e q", e=2),
                    in0=grad[m][:, half].rearrange("p (q e) -> p e q", e=2),
                    scalar=-COEF,
                    in1=lr_sb[:, m, half].rearrange("p (q e) -> p e q", e=2),
                    op0=ALU.mult,
                    op1=ALU.mult,
                )
            free_banks.append(m)

        def w_sum(m):
            total = next_bank([P, PACK, P], F32, "total")
            runs = [slice(2 * P * u + e, 2 * P * (u + 1), 2) for u in range(HALVES) for e in range(2)]
            for t, run in enumerate(runs):
                nc.tensor.matmul(
                    out=total[:, t, :], lhsT=w_sb[:, m, run], rhs=ident_bf16[:], start=(t == 0), stop=False
                )
            for t, run in enumerate(runs):
                nc.tensor.matmul(
                    out=total[:, t, :],
                    lhsT=step[m][:, t * P : (t + 1) * P],
                    rhs=ident_f32[:],
                    is_transpose=True,
                    start=False,
                    stop=(t == PACK - 1),
                )
            nc.scalar.copy(out=w_grouped[:, m], in_=total[:].rearrange("p t o -> p o t"))

        def w_quantise(m):
            o_cols = slice(m * P, (m + 1) * P)
            nc.vector.quantize_mx(
                out=w_codes[:, o_cols].bitcast(FP8X4),
                scales=w_scales[:, o_cols],
                in_=w_grouped[:, m].rearrange("p o t -> p (o t)"),
            )

        for c in range(CHUNKS):
            pair = regroup_pair(c)
            if c == CHUNKS - 1:
                update_bias()
                q_transpose(0)
            quantise_pair(c, pair)
            if c > 0:
                gradient(c - 1)
            if c == CHUNKS // 2:
                flipped_bias = flip_bias_rows()
            if c == CHUNKS // 2 + 1:
                copy_bias_cols(flipped_bias)
        q_transpose(1)
        q_transpose(2)
        gradient(CHUNKS - 1)
        q_quantise(0)
        w_step(0)
        w_step(1)
        w_sum(0)
        w_step(2)
        w_sum(1)
        w_step(3)
        w_quantise(0)
        w_sum(2)
        spread_bias()
        w_quantise(1)
        w_sum(3)
        q_quantise(1)
        w_quantise(2)
        q_transpose(3, (nc.vector.tensor_copy, nc.scalar.copy))
        w_quantise(3)
        q_quantise(2)
        q_transpose(4, (nc.vector.tensor_copy, nc.scalar.copy))
        product(0, 0)
        product(0, 1)
        q_quantise(3)
        product(0, 2)
        product(0, 3)
        q_transpose(5, (nc.vector.tensor_copy, nc.vector.tensor_copy))
        q_quantise(4)
        direct_slices = [(g, j) for g in DIRECT for j in range(PACK)]
        for r, g in enumerate(TRANSPOSED):
            now = direct_slices[: SHARES[r]]
            direct_slices = direct_slices[SHARES[r] :]
            last = r + 1 == len(TRANSPOSED)
            if not last:
                for m in range(BLOCKS - 1):
                    product(TRANSPOSED[r + 1], m)
            if r < 3:
                q_quantise(5 + r)
            if r < 2:
                add_bias(5, r, 5 + r)
            if r == 2:
                for i in range(4):
                    add_bias(6 + i // 2, i % 2, 7 - i if i == 0 else 5 - i)
            for slice_ in now:
                direct(*slice_)
            if not last:
                product(TRANSPOSED[r + 1], BLOCKS - 1)
            for j in range(PACK):
                if r > 0 and j == 3 or r > 2 and j == 1:
                    finish_on_scalar(g, j)
                else:
                    finish(g, j)
                if j == 1 and r < 2:
                    q_transpose(6 + r)
